import numpy as np
import ml_dtypes


def mxq(x, axis, fmt="e4m3"):
    dtype, down = {"e4m3": (ml_dtypes.float8_e4m3fn, 7), "e5m2": (ml_dtypes.float8_e5m2, 14)}[fmt]
    v = np.moveaxis(np.asarray(x, np.float32).astype(ml_dtypes.bfloat16).astype(np.float64), axis, -1)
    blocks = v.reshape(v.shape[:-1] + (-1, 32))
    amax = np.abs(blocks).max(-1, keepdims=True)
    byte = np.maximum(np.where(amax > 0, np.frexp(amax)[1] - 1 + 127, 0) - down, 1)
    scale = np.exp2(byte - 127.0)
    codes = (blocks / scale).astype(np.float32).astype(dtype).astype(np.float64)
    return np.moveaxis((codes * scale).reshape(v.shape), -1, axis)


WIDE = False


def mx_kscale(k):
    if not WIDE:
        return np.ones(k)
    levels = np.array([10, -10, 5, -5, 0])
    a = np.random.permutation(np.resize(levels, k // 512 * 4)).reshape(k // 512, 4)
    idx = np.arange(k)
    return np.exp2(a[idx // 512, idx % 128 // 32])


BF16 = ml_dtypes.bfloat16


def bf(x):
    return np.asarray(x, np.float32).astype(BF16)


def f64(x):
    return np.asarray(x).astype(np.float64)


B, D, C, NP, NS = 4096, 512, 512, 1024, 512
ALPHA_NEG = 1.0 / 10.0


def relu(v):
    return np.maximum(v, 0.0)


def setup_inputs():
    t = mx_kscale(NP)
    u = mx_kscale(NS)
    return {
        "x_batch": bf(np.random.uniform(size=(B, D))),
        "predicted": bf(np.random.standard_normal((B, D))),
        "r_som": bf(np.maximum(np.random.standard_normal((B, NS)), 0.0) * 1.1 * u),
        "r_neg_batch": bf(np.random.uniform(size=(B, D)) * 0.5),
        "W_pv1_ff": bf(np.random.standard_normal((NP, D)) * 1.5 / np.sqrt(D) * t[:, None]),
        "W_inh_pe_neg": bf(np.random.standard_normal((D, NP)) * 1.2 / np.sqrt(NP) / t),
        "W_som_dend": bf(np.random.standard_normal((D, NS)) * 0.9 / np.sqrt(NS) / u),
    }


def reference(x_batch, predicted, r_som, r_neg_batch, W_pv1_ff, W_inh_pe_neg, W_som_dend):
    xf, pf = f64(x_batch), f64(predicted)
    r_pv1 = relu(mxq(xf, 1, "e4m3") @ mxq(f64(W_pv1_ff), 1, "e4m3").T)
    inh_pv = mxq(r_pv1, 1, "e4m3") @ mxq(f64(W_inh_pe_neg), 1, "e4m3").T
    inh_som = mxq(f64(r_som), 1, "e4m3") @ mxq(f64(W_som_dend), 1, "e4m3").T
    pe_neg = relu(pf - xf - inh_pv - inh_som)
    return (1.0 - ALPHA_NEG) * f64(r_neg_batch) + ALPHA_NEG * pe_neg

@@ -1,0 +1,286 @@
+from contextlib import ExitStack
+
+import concourse.mybir as mybir
+from concourse.masks import make_identity
+
+F32 = mybir.dt.float32
+BF16 = mybir.dt.bfloat16
+U32 = mybir.dt.uint32
+U8 = mybir.dt.uint8
+FP8X4 = mybir.dt.float8_e4m3fn_x4
+ALU = mybir.AluOpType
+ACT = mybir.ActivationFunctionType
+
+P = 128
+B, D, NP, NS = 4096, 512, 1024, 512
+FLOPS = 2 * B * (D * NP + NP * D + NS * D)
+NU = B // P
+GROUPS = (2, 2, 4, 4, 4, 4, 4, 4, 2, 1, 1)
+LT = 2
+LD = 3
+LA = -1
+LEAD = 4
+PINNED = True
+
+
+def tile_pecircuits_pb_t_kernel(
+    tc, x_batch, predicted, r_som, r_neg_batch, W_pv1_ff, W_inh_pe_neg, W_som_dend, out
+):
+    nc = tc.nc
+    first = [sum(GROUPS[:i]) for i in range(len(GROUPS))]
+    unit_group = {}
+    for gi, t in enumerate(GROUPS):
+        for j in range(t):
+            unit_group[first[gi] + j] = (gi, j)
+
+    with ExitStack() as ctx:
+        const = ctx.enter_context(tc.tile_pool(name="const", bufs=1))
+        inp = ctx.enter_context(tc.tile_pool(name="inp", bufs=4))
+        grp = ctx.enter_context(tc.tile_pool(name="grp", bufs=3))
+        cod = ctx.enter_context(tc.tile_pool(name="cod", bufs=LD + 3))
+        epi = ctx.enter_context(tc.tile_pool(name="epi", bufs=4))
+        ps_t = ctx.enter_context(tc.psum_pool(name="ps_t", bufs=2))
+        ps_c = ctx.enter_context(tc.psum_pool(name="ps_c", bufs=4))
+        ps_d = ctx.enter_context(tc.psum_pool(name="ps_d", bufs=2))
+
+        ident = const.tile([P, P], F32)
+        make_identity(nc, ident[:])
+        if PINNED:
+            ctx.enter_context(tc.manual_schedule())
+
+        def gview(ap, gi):
+            t = GROUPS[gi]
+            r0 = P * first[gi]
+            return ap[r0 : r0 + P * t, :].rearrange("(p t) d -> p (t d)", t=t)
+
+        srcs = {"x": x_batch, "som": r_som, "pr": predicted, "rn": r_neg_batch}
+        tiles = {}
+
+        def load(gi, which):
+            t = inp.tile([P, GROUPS[gi] * D], BF16, name="in_" + which)
+            nc.sync.dma_start(out=t[:], in_=gview(srcs[which], gi))
+            tiles[(which, gi)] = t
+
+        def t_bank(blocks):
+            bank = ps_t.tile([P, 2, 2, P], F32)
+            for l, (src32, off) in enumerate(blocks):
+                for u in range(2):
+                    o = off + P * u
+                    nc.tensor.transpose(bank[:, l, u, :], src32[:, o : o + P], ident[:])
+            return bank
+
+        def t_copy(bank, dst32, on_vector):
+            dst = dst32.rearrange("p (l j u) -> p l j u", l=2, u=2)
+            src = bank[:].rearrange("p l u j -> p l j u")
+            if on_vector:
+                nc.vector.tensor_copy(out=dst, in_=src)
+            else:
+                nc.scalar.copy(out=dst, in_=src)
+
+        def quantise(codes, scales, grouped):
+            nc.vector.quantize_mx(out=codes.bitcast(FP8X4), scales=scales, in_=grouped)
+
+        w1_sb = const.tile([P, 4096], BF16)
+        w2_sb = const.tile([P, 4096], BF16)
+        w3_sb = const.tile([P, 2048], BF16)
+        w1g = const.tile([P, 4096], BF16, align_bytes=64)
+        w2g = const.tile([P, 4096], BF16, align_bytes=64)
+        w3g = const.tile([P, 2048], BF16, align_bytes=64)
+        w1c = const.tile([P, 1024], U32, align_bytes=64)
+        w2c = const.tile([P, 1024], U32, align_bytes=64)
+        w3c = const.tile([P, 512], U32, align_bytes=64)
+        w1s = const.tile([P, 1024], U8, align_bytes=64)
+        w2s = const.tile([P, 1024], U8, align_bytes=64)
+        w3s = const.tile([P, 512], U8, align_bytes=64)
+
+        def load_w1(g):
+            nc.sync.dma_start(
+                out=w1_sb[:, 2048 * g : 2048 * g + 2048].rearrange("p (a r) -> p a r", a=2),
+                in_=W_pv1_ff[512 * g : 512 * g + 512, :].rearrange("(a p e) k -> p a (e k)", a=2, p=P, e=2),
+            )
+
+        def load_w2():
+            nc.sync.dma_start(
+                out=w2_sb[:].rearrange("p (a r) -> p a r", a=4),
+                in_=W_inh_pe_neg.rearrange("(a p) k -> p a k", p=P),
+            )
+
+        def load_w3():
+            nc.sync.dma_start(
+                out=w3_sb[:].rearrange("p (a r) -> p a r", a=4),
+                in_=W_som_dend.rearrange("(a p) k -> p a k", p=P),
+            )
+
+        def prep_w(src, grouped, codes, scales, offs, q):
+            s32 = src[:].bitcast(F32)
+            g32 = grouped[:].bitcast(F32)
+            for h in range(2):
+                bank = t_bank([(s32, offs[2 * h]), (s32, offs[2 * h + 1])])
+                o = 1024 * q + 512 * h
+                t_copy(bank, g32[:, o : o + 512], h == 0)
+            quantise(
+                codes[:, 512 * q : 512 * q + 512],
+                scales[:, 512 * q : 512 * q + 512],
+                grouped[:, 2048 * q : 2048 * q + 2048],
+            )
+
+        def prep_w1(g):
+            prep_w(w1_sb, w1g, w1c, w1s, [1024 * g + 256 * n for n in range(4)], g)
+
+        def prep_w2(g):
+            prep_w(w2_sb, w2g, w2c, w2s, [512 * n + 256 * g for n in range(4)], g)
+
+        def prep_w3():
+            prep_w(w3_sb, w3g, w3c, w3s, [256 * n for n in range(4)], 0)
+
+        def ok(u):
+            return 0 <= u < NU
+
+        def ph_t(u):
+            gi, j = unit_group[u]
+            tiles[("tb", u)] = t_bank(
+                [(tiles[("x", gi)][:].bitcast(F32), 256 * j), (tiles[("som", gi)][:].bitcast(F32), 256 * j)]
+            )
+
+        def ph_tc(u):
+            g = grp.tile([P, 1024], BF16, name="g_xs", align_bytes=64)
+            t_copy(tiles[("tb", u)], g[:].bitcast(F32), False)
+            tiles[("gxs", u)] = g
+
+        def ph_q(u):
+            codes = cod.tile([P, 256], U32, name="c_xs", align_bytes=64, bufs=LT + LD + 3)
+            scales = cod.tile([P, 256], U8, name="s_xs", align_bytes=64, bufs=LT + LD + 3)
+            quantise(codes[:], scales[:], tiles[("gxs", u)][:])
+            tiles[("cxs", u)] = codes
+            tiles[("sxs", u)] = scales
+
+        def ph_a(u):
+            gi, j = unit_group[u]
+            if j == 0:
+                e_new = epi.tile([P, GROUPS[gi] * D], F32, name="e")
+                tiles[("e", gi)] = e_new
+            e = tiles[("e", gi)]
+            sl = slice(D * j, D * j + D)
+            nc.vector.tensor_tensor(
+                out=e[:, sl], in0=tiles[("pr", gi)][:, sl], in1=tiles[("x", gi)][:, sl], op=ALU.subtract
+            )
+
+        def ph_c(u):
+            xc, xs = tiles[("cxs", u)], tiles[("sxs", u)]
+            for g in range(2):
+                bank = ps_c.tile([P, 4, P], F32)
+                for t in range(4):
+                    m = P * (4 * g + t)
+                    nc.tensor.matmul_mx(
+                        out=bank[:, t, :],
+                        lhsT=w1c[:, m : m + P].bitcast(FP8X4),
+                        lhsT_scale=w1s[:, m : m + P],
+                        rhs=xc[:, 0:P].bitcast(FP8X4),
+                        rhs_scale=xs[:, 0:P],
+                        start=True,
+                        stop=True,
+                    )
+                tiles[("cb", u, g)] = bank
+
+        def ph_r(u):
+            rg = grp.tile([P, 1024], BF16, name="g_r", align_bytes=64)
+            for g in range(2):
+                nc.scalar.activation(
+                    out=rg[:, 512 * g : 512 * g + 512].rearrange("p (j t) -> p j t", t=4),
+                    in_=tiles[("cb", u, g)][:].rearrange("p t j -> p j t"),
+                    func=ACT.Relu,
+                )
+            tiles[("rg", u)] = rg
+
+        def ph_qr(u):
+            rc = cod.tile([P, 256], U32, name="c_r", align_bytes=64)
+            rs = cod.tile([P, 256], U8, name="s_r", align_bytes=64)
+            quantise(rc[:], rs[:], tiles[("rg", u)][:])
+            tiles[("rc", u)] = rc
+            tiles[("rs", u)] = rs
+
+        def ph_d(u):
+            rc, rs = tiles[("rc", u)], tiles[("rs", u)]
+            sc, ss = tiles[("cxs", u)], tiles[("sxs", u)]
+            acc = ps_d.tile([P, D], F32)
+            passes = ((sc, ss, P, w3c, w3s, 0), (rc, rs, 0, w2c, w2s, 0), (rc, rs, P, w2c, w2s, 512))
+            for i, (lc, ls, lo, wc, ws, wo) in enumerate(passes):
+                nc.tensor.matmul_mx(
+                    out=acc[:],
+                    lhsT=lc[:, lo : lo + P].bitcast(FP8X4),
+                    lhsT_scale=ls[:, lo : lo + P],
+                    rhs=wc[:, wo : wo + 512].bitcast(FP8X4),
+                    rhs_scale=ws[:, wo : wo + 512],
+                    start=(i == 0),
+                    stop=(i == 2),
+                )
+            tiles[("acc", u)] = acc
+
+        def e_slice(u):
+            gi, j = unit_group[u]
+            return tiles[("e", gi)][:, D * j : D * j + D]
+
+        def ph_b(u):
+            nc.vector.tensor_tensor(out=e_slice(u), in0=e_slice(u), in1=tiles[("acc", u)][:], op=ALU.subtract)
+
+        def ph_relu(u):
+            nc.scalar.activation(out=e_slice(u), in_=e_slice(u), func=ACT.Relu, scale=0.1)
+
+        def ph_out(u):
+            gi, j = unit_group[u]
+            nc.vector.scalar_tensor_tensor(
+                out=e_slice(u), in0=tiles[("rn", gi)][:, D * j : D * j + D], scalar=0.9, in1=e_slice(u),
+                op0=ALU.mult, op1=ALU.add,
+            )
+            if j == GROUPS[gi] - 1:
+                nc.sync.dma_start(out=gview(out, gi), in_=tiles[("e", gi)][:])
+
+        load(0, "x")
+        load(0, "som")
+        load_w1(0)
+        load_w1(1)
+        load(1, "x")
+        load(1, "som")
+        load(0, "pr")
+        load_w3()
+        load_w2()
+        load(1, "pr")
+        load(0, "rn")
+        load(1, "rn")
+        loaded = 2
+
+        for i in range(-LT, NU + LD + 2):
+            while loaded < len(GROUPS) and first[loaded] - LT - LEAD <= i:
+                for which in ("x", "som", "pr", "rn"):
+                    load(loaded, which)
+                loaded += 1
+            if i == 0:
+                prep_w1(0)
+                prep_w1(1)
+            if i == LD:
+                prep_w3()
+                prep_w2(0)
+                prep_w2(1)
+            if ok(i):
+                ph_c(i)
+                ph_r(i)
+            if (i + LT) % 2 == 0:
+                for u in (i + LT, i + LT + 1):
+                    if ok(u):
+                        ph_t(u)
+            if ok(i + LT):
+                ph_tc(i + LT)
+            if ok(i - LD):
+                ph_d(i - LD)
+            if ok(i - LD - 1):
+                ph_relu(i - LD - 1)
+            if ok(i + LA):
+                ph_a(i + LA)
+            if ok(i):
+                ph_qr(i)
+            if ok(i + LT):
+                ph_q(i + LT)
+            if ok(i - LD):
+                ph_b(i - LD)
+            if ok(i - LD - 1):
+                ph_out(i - LD - 1)

@@ -15,11 +15,14 @@ P = 128
 B, D, NP, NS = 4096, 512, 1024, 512
 FLOPS = 2 * B * (D * NP + NP * D + NS * D)
 NU = B // P
-GROUPS = (2, 2, 4, 4, 4, 4, 4, 4, 2, 1, 1)
-LT = 2
-LD = 3
-LA = -1
+GROUPS = (2, 2, 2, 2, 4, 4, 4, 4, 4, 2, 1, 1)
+O_TC, O_Q, O_C, O_R, O_QR, O_D, O_B, O_RELU, O_OUT = 1, 2, 3, 4, 5, 9, 10, 11, 12
+O_A = 1
 LEAD = 4
+NBUF = {"x": 4, "som": 4, "pr": 4, "rn": 4}
+LAST_USE = {"x": O_A, "som": 0, "pr": O_A, "rn": O_OUT}
+FIRST_USE = {"x": 0, "som": 0, "pr": O_A, "rn": O_OUT - 4}
+TC_ON_VECTOR = ()
 PINNED = True
 
 
@@ -37,8 +40,8 @@ def tile_pecircuits_pb_t_kernel(
         const = ctx.enter_context(tc.tile_pool(name="const", bufs=1))
         inp = ctx.enter_context(tc.tile_pool(name="inp", bufs=4))
         grp = ctx.enter_context(tc.tile_pool(name="grp", bufs=3))
-        cod = ctx.enter_context(tc.tile_pool(name="cod", bufs=LD + 3))
-        epi = ctx.enter_context(tc.tile_pool(name="epi", bufs=4))
+        cod = ctx.enter_context(tc.tile_pool(name="cod", bufs=3))
+        epi = ctx.enter_context(tc.tile_pool(name="epi", bufs=6))
         ps_t = ctx.enter_context(tc.psum_pool(name="ps_t", bufs=2))
         ps_c = ctx.enter_context(tc.psum_pool(name="ps_c", bufs=4))
         ps_d = ctx.enter_context(tc.psum_pool(name="ps_d", bufs=2))
@@ -57,12 +60,12 @@ def tile_pecircuits_pb_t_kernel(
         tiles = {}
 
         def load(gi, which):
-            t = inp.tile([P, GROUPS[gi] * D], BF16, name="in_" + which)
+            t = inp.tile([P, GROUPS[gi] * D], BF16, name="in_" + which, bufs=NBUF[which])
             nc.sync.dma_start(out=t[:], in_=gview(srcs[which], gi))
             tiles[(which, gi)] = t
 
-        def t_bank(blocks):
-            bank = ps_t.tile([P, 2, 2, P], F32)
+        def t_bank(pool, tag, blocks):
+            bank = pool.tile([P, 2, 2, P], F32, name=tag, tag=tag)
             for l, (src32, off) in enumerate(blocks):
                 for u in range(2):
                     o = off + P * u
@@ -111,27 +114,30 @@ def tile_pecircuits_pb_t_kernel(
                 in_=W_som_dend.rearrange("(a p) k -> p a k", p=P),
             )
 
-        def prep_w(src, grouped, codes, scales, offs, q):
+        weights = {
+            "w1": (ps_c, "cb", w1_sb, w1g, w1c, w1s, lambda q: [1024 * q + 256 * n for n in range(4)]),
+            "w2": (ps_d, "db", w2_sb, w2g, w2c, w2s, lambda q: [512 * n + 256 * q for n in range(4)]),
+            "w3": (ps_d, "db", w3_sb, w3g, w3c, w3s, lambda q: [256 * n for n in range(4)]),
+        }
+
+        def w_t(key, q, h):
+            pool, tag, src, grouped, codes, scales, offs_of = weights[key]
             s32 = src[:].bitcast(F32)
-            g32 = grouped[:].bitcast(F32)
-            for h in range(2):
-                bank = t_bank([(s32, offs[2 * h]), (s32, offs[2 * h + 1])])
-                o = 1024 * q + 512 * h
-                t_copy(bank, g32[:, o : o + 512], h == 0)
+            offs = offs_of(q)
+            tiles[("wb", key, q, h)] = t_bank(pool, tag, [(s32, offs[2 * h]), (s32, offs[2 * h + 1])])
+
+        def w_c(key, q, h, on_vector):
+            grouped = weights[key][3]
+            o = 1024 * q + 512 * h
+            t_copy(tiles[("wb", key, q, h)], grouped[:].bitcast(F32)[:, o : o + 512], on_vector)
+
+        def w_q(key, q):
+            pool, tag, src, grouped, codes, scales, offs_of = weights[key]
             quantise(
                 codes[:, 512 * q : 512 * q + 512],
                 scales[:, 512 * q : 512 * q + 512],
                 grouped[:, 2048 * q : 2048 * q + 2048],
             )
-
-        def prep_w1(g):
-            prep_w(w1_sb, w1g, w1c, w1s, [1024 * g + 256 * n for n in range(4)], g)
-
-        def prep_w2(g):
-            prep_w(w2_sb, w2g, w2c, w2s, [512 * n + 256 * g for n in range(4)], g)
-
-        def prep_w3():
-            prep_w(w3_sb, w3g, w3c, w3s, [256 * n for n in range(4)], 0)
 
         def ok(u):
             return 0 <= u < NU
@@ -139,17 +145,18 @@ def tile_pecircuits_pb_t_kernel(
         def ph_t(u):
             gi, j = unit_group[u]
             tiles[("tb", u)] = t_bank(
-                [(tiles[("x", gi)][:].bitcast(F32), 256 * j), (tiles[("som", gi)][:].bitcast(F32), 256 * j)]
+                ps_t, "tb",
+                [(tiles[("x", gi)][:].bitcast(F32), 256 * j), (tiles[("som", gi)][:].bitcast(F32), 256 * j)],
             )
 
         def ph_tc(u):
             g = grp.tile([P, 1024], BF16, name="g_xs", align_bytes=64)
-            t_copy(tiles[("tb", u)], g[:].bitcast(F32), False)
+            t_copy(tiles[("tb", u)], g[:].bitcast(F32), u in TC_ON_VECTOR)
             tiles[("gxs", u)] = g
 
         def ph_q(u):
-            codes = cod.tile([P, 256], U32, name="c_xs", align_bytes=64, bufs=LT + LD + 3)
-            scales = cod.tile([P, 256], U8, name="s_xs", align_bytes=64, bufs=LT + LD + 3)
+            codes = cod.tile([P, 256], U32, name="c_xs", align_bytes=64, bufs=O_D - O_Q + 2)
+            scales = cod.tile([P, 256], U8, name="s_xs", align_bytes=64, bufs=O_D - O_Q + 2)
             quantise(codes[:], scales[:], tiles[("gxs", u)][:])
             tiles[("cxs", u)] = codes
             tiles[("sxs", u)] = scales
@@ -168,7 +175,7 @@ def tile_pecircuits_pb_t_kernel(
         def ph_c(u):
             xc, xs = tiles[("cxs", u)], tiles[("sxs", u)]
             for g in range(2):
-                bank = ps_c.tile([P, 4, P], F32)
+                bank = ps_c.tile([P, 4, P], F32, name="cb", tag="cb")
                 for t in range(4):
                     m = P * (4 * g + t)
                     nc.tensor.matmul_mx(
@@ -193,8 +200,8 @@ def tile_pecircuits_pb_t_kernel(
             tiles[("rg", u)] = rg
 
         def ph_qr(u):
-            rc = cod.tile([P, 256], U32, name="c_r", align_bytes=64)
-            rs = cod.tile([P, 256], U8, name="s_r", align_bytes=64)
+            rc = cod.tile([P, 256], U32, name="c_r", align_bytes=64, bufs=O_D - O_QR + 2)
+            rs = cod.tile([P, 256], U8, name="s_r", align_bytes=64, bufs=O_D - O_QR + 2)
             quantise(rc[:], rs[:], tiles[("rg", u)][:])
             tiles[("rc", u)] = rc
             tiles[("rs", u)] = rs
@@ -202,7 +209,7 @@ def tile_pecircuits_pb_t_kernel(
         def ph_d(u):
             rc, rs = tiles[("rc", u)], tiles[("rs", u)]
             sc, ss = tiles[("cxs", u)], tiles[("sxs", u)]
-            acc = ps_d.tile([P, D], F32)
+            acc = ps_d.tile([P, D], F32, name="db", tag="db")
             passes = ((sc, ss, P, w3c, w3s, 0), (rc, rs, 0, w2c, w2s, 0), (rc, rs, P, w2c, w2s, 512))
             for i, (lc, ls, lo, wc, ws, wo) in enumerate(passes):
                 nc.tensor.matmul_mx(
@@ -237,50 +244,87 @@ def tile_pecircuits_pb_t_kernel(
 
         load(0, "x")
         load(0, "som")
+        load(0, "pr")
         load_w1(0)
         load_w1(1)
         load(1, "x")
         load(1, "som")
-        load(0, "pr")
+        load(1, "pr")
+        load(2, "x")
+        load(2, "som")
+        load(2, "pr")
         load_w3()
         load_w2()
-        load(1, "pr")
-        load(0, "rn")
-        load(1, "rn")
-        loaded = 2
+        head_loads = {(0, "x"), (0, "som"), (0, "pr"), (1, "x"), (1, "som"), (1, "pr"), (2, "x"), (2, "som"), (2, "pr")}
+        loads_at = {}
+        for gi in range(len(GROUPS)):
+            for which in ("x", "som", "pr", "rn"):
+                if (gi, which) in head_loads:
+                    continue
+                k = first[gi] + FIRST_USE[which] - LEAD
+                old = gi - NBUF[which]
+                if old >= 0:
+                    k = max(k, first[old] + GROUPS[old] - 1 + LAST_USE[which] + 1)
+                k = max(k, 0)
+                if k not in loads_at:
+                    loads_at[k] = []
+                loads_at[k].append((gi, which))
 
-        for i in range(-LT, NU + LD + 2):
-            while loaded < len(GROUPS) and first[loaded] - LT - LEAD <= i:
-                for which in ("x", "som", "pr", "rn"):
-                    load(loaded, which)
-                loaded += 1
-            if i == 0:
-                prep_w1(0)
-                prep_w1(1)
-            if i == LD:
-                prep_w3()
-                prep_w2(0)
-                prep_w2(1)
-            if ok(i):
-                ph_c(i)
-                ph_r(i)
-            if (i + LT) % 2 == 0:
-                for u in (i + LT, i + LT + 1):
+        for k in range(0, NU + O_OUT):
+            for gi, which in loads_at.get(k, []):
+                load(gi, which)
+            if ok(k - O_TC):
+                ph_tc(k - O_TC)
+            if ok(k - O_C):
+                ph_c(k - O_C)
+            if ok(k - O_D):
+                ph_d(k - O_D)
+            if k % 2 == 0:
+                for u in (k, k + 1):
                     if ok(u):
                         ph_t(u)
-            if ok(i + LT):
-                ph_tc(i + LT)
-            if ok(i - LD):
-                ph_d(i - LD)
-            if ok(i - LD - 1):
-                ph_relu(i - LD - 1)
-            if ok(i + LA):
-                ph_a(i + LA)
-            if ok(i):
-                ph_qr(i)
-            if ok(i + LT):
-                ph_q(i + LT)
-            if ok(i - LD):
-                ph_b(i - LD)
-            if ok(i - LD - 1):
-                ph_out(i - LD - 1)
+            if ok(k - O_R):
+                ph_r(k - O_R)
+            if ok(k - O_RELU):
+                ph_relu(k - O_RELU)
+            if ok(k - O_Q):
+                ph_q(k - O_Q)
+            if ok(k - O_QR):
+                ph_qr(k - O_QR)
+            if ok(k - O_B):
+                ph_b(k - O_B)
+            if ok(k - O_OUT):
+                ph_out(k - O_OUT)
+            if ok(k - O_A):
+                ph_a(k - O_A)
+            if k == 1:
+                w_t("w1", 0, 0)
+                w_t("w1", 0, 1)
+                w_t("w1", 1, 0)
+                w_t("w1", 1, 1)
+                w_c("w1", 0, 0, True)
+                w_c("w1", 0, 1, False)
+                w_q("w1", 0)
+                w_c("w1", 1, 0, True)
+                w_c("w1", 1, 1, False)
+                w_q("w1", 1)
+            if k == 4:
+                w_t("w3", 0, 0)
+                w_t("w3", 0, 1)
+            if k == 5:
+                w_c("w3", 0, 0, True)
+                w_c("w3", 0, 1, False)
+                w_t("w2", 0, 0)
+                w_t("w2", 0, 1)
+            if k == 6:
+                w_q("w3", 0)
+                w_c("w2", 0, 0, True)
+                w_c("w2", 0, 1, False)
+                w_t("w2", 1, 0)
+                w_t("w2", 1, 1)
+            if k == 7:
+                w_q("w2", 0)
+                w_c("w2", 1, 0, True)
+                w_c("w2", 1, 1, False)
+            if k == 8:
+                w_q("w2", 1)

@@ -20,9 +20,11 @@ O_TC, O_Q, O_C, O_R, O_QR, O_D, O_B, O_RELU, O_OUT = 1, 2, 3, 4, 5, 9, 10, 11, 1
 O_A = 1
 LEAD = 4
 NBUF = {"x": 4, "som": 4, "pr": 4, "rn": 4}
-LAST_USE = {"x": O_A, "som": 0, "pr": O_A, "rn": O_OUT}
+LAST_USE = {"x": max(O_A, 0), "som": 0, "pr": max(O_A, 0), "rn": O_OUT}
 FIRST_USE = {"x": 0, "som": 0, "pr": O_A, "rn": O_OUT - 4}
 TC_ON_VECTOR = ()
+GP_A = ()
+R_ON_VECTOR = ()
 PINNED = True
 
 
@@ -163,14 +165,11 @@ def tile_pecircuits_pb_t_kernel(
 
         def ph_a(u):
             gi, j = unit_group[u]
-            if j == 0:
-                e_new = epi.tile([P, GROUPS[gi] * D], F32, name="e")
-                tiles[("e", gi)] = e_new
-            e = tiles[("e", gi)]
-            sl = slice(D * j, D * j + D)
-            nc.vector.tensor_tensor(
-                out=e[:, sl], in0=tiles[("pr", gi)][:, sl], in1=tiles[("x", gi)][:, sl], op=ALU.subtract
-            )
+            if j != 0:
+                return
+            e = epi.tile([P, GROUPS[gi] * D], F32, name="e")
+            tiles[("e", gi)] = e
+            nc.vector.tensor_tensor(out=e[:], in0=tiles[("pr", gi)][:], in1=tiles[("x", gi)][:], op=ALU.subtract)
 
         def ph_c(u):
             xc, xs = tiles[("cxs", u)], tiles[("sxs", u)]
@@ -192,11 +191,12 @@ def tile_pecircuits_pb_t_kernel(
         def ph_r(u):
             rg = grp.tile([P, 1024], BF16, name="g_r", align_bytes=64)
             for g in range(2):
-                nc.scalar.activation(
-                    out=rg[:, 512 * g : 512 * g + 512].rearrange("p (j t) -> p j t", t=4),
-                    in_=tiles[("cb", u, g)][:].rearrange("p t j -> p j t"),
-                    func=ACT.Relu,
-                )
+                dst = rg[:, 512 * g : 512 * g + 512].rearrange("p (j t) -> p j t", t=4)
+                src = tiles[("cb", u, g)][:].rearrange("p t j -> p j t")
+                if (u, g) in R_ON_VECTOR:
+                    nc.vector.tensor_scalar_max(out=dst, in0=src, scalar1=0.0)
+                else:
+                    nc.scalar.activation(out=dst, in_=src, func=ACT.Relu)
             tiles[("rg", u)] = rg
 
         def ph_qr(u):
@@ -223,24 +223,33 @@ def tile_pecircuits_pb_t_kernel(
                 )
             tiles[("acc", u)] = acc
 
-        def e_slice(u):
+        def e_slice(u, n=1):
             gi, j = unit_group[u]
-            return tiles[("e", gi)][:, D * j : D * j + D]
+            return tiles[("e", gi)][:, D * j : D * (j + n)]
+
+        def runs(u):
+            if u % 2 == 0:
+                return ()
+            if unit_group[u - 1][0] == unit_group[u][0]:
+                return ((u - 1, 2),)
+            return ((u - 1, 1), (u, 1))
 
         def ph_b(u):
             nc.vector.tensor_tensor(out=e_slice(u), in0=e_slice(u), in1=tiles[("acc", u)][:], op=ALU.subtract)
 
         def ph_relu(u):
-            nc.scalar.activation(out=e_slice(u), in_=e_slice(u), func=ACT.Relu, scale=0.1)
+            for v, n in runs(u):
+                nc.scalar.activation(out=e_slice(v, n), in_=e_slice(v, n), func=ACT.Relu, scale=0.1)
 
         def ph_out(u):
-            gi, j = unit_group[u]
-            nc.vector.scalar_tensor_tensor(
-                out=e_slice(u), in0=tiles[("rn", gi)][:, D * j : D * j + D], scalar=0.9, in1=e_slice(u),
-                op0=ALU.mult, op1=ALU.add,
-            )
-            if j == GROUPS[gi] - 1:
-                nc.sync.dma_start(out=gview(out, gi), in_=tiles[("e", gi)][:])
+            for v, n in runs(u):
+                gi, j = unit_group[v]
+                nc.vector.scalar_tensor_tensor(
+                    out=e_slice(v, n), in0=tiles[("rn", gi)][:, D * j : D * (j + n)], scalar=0.9, in1=e_slice(v, n),
+                    op0=ALU.mult, op1=ALU.add,
+                )
+                if j + n == GROUPS[gi]:
+                    nc.sync.dma_start(out=gview(out, gi), in_=tiles[("e", gi)][:])
 
         load(0, "x")
         load(0, "som")

@@ -16,16 +16,15 @@ B, D, NP, NS = 4096, 512, 1024, 512
 FLOPS = 2 * B * (D * NP + NP * D + NS * D)
 NU = B // P
 GROUPS = (2, 2, 2, 2, 4, 4, 4, 4, 4, 2, 1, 1)
-O_TC, O_Q, O_C, O_R, O_QR, O_D, O_B, O_RELU, O_OUT = 1, 2, 3, 4, 5, 9, 10, 11, 12
-O_A = 1
+O_TC, O_Q, O_C, O_R, O_QR, O_D, O_B, O_OUT = 1, 2, 4, 5, 6, 7, 8, 9
+E_PAIRS = 3
+O_AG = O_OUT - 2 * E_PAIRS
+O_AV = O_AG + 1
+RV = 256
 LEAD = 4
 NBUF = {"x": 4, "som": 4, "pr": 4, "rn": 4}
-LAST_USE = {"x": max(O_A, 0), "som": 0, "pr": max(O_A, 0), "rn": O_OUT}
-FIRST_USE = {"x": 0, "som": 0, "pr": O_A, "rn": O_OUT - 4}
-TC_ON_VECTOR = ()
-GP_A = ()
-R_ON_VECTOR = ()
-PINNED = True
+LAST_USE = {"x": 5, "som": 0, "pr": 5, "rn": O_OUT}
+FIRST_USE = {"x": 0, "som": 0, "pr": 0, "rn": O_OUT - 4}
 
 
 def tile_pecircuits_pb_t_kernel(
@@ -50,8 +49,7 @@ def tile_pecircuits_pb_t_kernel(
 
         ident = const.tile([P, P], F32)
         make_identity(nc, ident[:])
-        if PINNED:
-            ctx.enter_context(tc.manual_schedule())
+        ctx.enter_context(tc.manual_schedule())
 
         def gview(ap, gi):
             t = GROUPS[gi]
@@ -153,7 +151,7 @@ def tile_pecircuits_pb_t_kernel(
 
         def ph_tc(u):
             g = grp.tile([P, 1024], BF16, name="g_xs", align_bytes=64)
-            t_copy(tiles[("tb", u)], g[:].bitcast(F32), u in TC_ON_VECTOR)
+            t_copy(tiles[("tb", u)], g[:].bitcast(F32), False)
             tiles[("gxs", u)] = g
 
         def ph_q(u):
@@ -163,13 +161,15 @@ def tile_pecircuits_pb_t_kernel(
             tiles[("cxs", u)] = codes
             tiles[("sxs", u)] = scales
 
-        def ph_a(u):
+        def ph_a(u, engine):
+            if ("e", u - u % 2) not in tiles:
+                e = epi.tile([P, 2 * D], F32, name="e", bufs=E_PAIRS)
+                tiles[("e", u - u % 2)] = e
             gi, j = unit_group[u]
-            if j != 0:
-                return
-            e = epi.tile([P, GROUPS[gi] * D], F32, name="e")
-            tiles[("e", gi)] = e
-            nc.vector.tensor_tensor(out=e[:], in0=tiles[("pr", gi)][:], in1=tiles[("x", gi)][:], op=ALU.subtract)
+            cols = slice(D * j, D * j + D)
+            engine.tensor_tensor(
+                out=e_slice(u), in0=tiles[("pr", gi)][:, cols], in1=tiles[("x", gi)][:, cols], op=ALU.subtract
+            )
 
         def ph_c(u):
             xc, xs = tiles[("cxs", u)], tiles[("sxs", u)]
@@ -193,10 +193,7 @@ def tile_pecircuits_pb_t_kernel(
             for g in range(2):
                 dst = rg[:, 512 * g : 512 * g + 512].rearrange("p (j t) -> p j t", t=4)
                 src = tiles[("cb", u, g)][:].rearrange("p t j -> p j t")
-                if (u, g) in R_ON_VECTOR:
-                    nc.vector.tensor_scalar_max(out=dst, in0=src, scalar1=0.0)
-                else:
-                    nc.scalar.activation(out=dst, in_=src, func=ACT.Relu)
+                nc.scalar.activation(out=dst, in_=src, func=ACT.Relu)
             tiles[("rg", u)] = rg
 
         def ph_qr(u):
@@ -224,47 +221,56 @@ def tile_pecircuits_pb_t_kernel(
             tiles[("acc", u)] = acc
 
         def e_slice(u, n=1):
-            gi, j = unit_group[u]
-            return tiles[("e", gi)][:, D * j : D * (j + n)]
+            j = u % 2
+            return tiles[("e", u - j)][:, D * j : D * (j + n)]
 
         def runs(u):
-            if u % 2 == 0:
-                return ()
-            if unit_group[u - 1][0] == unit_group[u][0]:
-                return ((u - 1, 2),)
-            return ((u - 1, 1), (u, 1))
+            if unit_group[u][0] == unit_group[u + 1][0]:
+                return ((u, 2),)
+            return ((u, 1), (u + 1, 1))
 
         def ph_b(u):
-            nc.vector.tensor_tensor(out=e_slice(u), in0=e_slice(u), in1=tiles[("acc", u)][:], op=ALU.subtract)
+            for v in (u, u + 1):
+                nc.vector.tensor_tensor(out=e_slice(v), in0=e_slice(v), in1=tiles[("acc", v)][:], op=ALU.subtract)
 
         def ph_relu(u):
-            for v, n in runs(u):
-                nc.scalar.activation(out=e_slice(v, n), in_=e_slice(v, n), func=ACT.Relu, scale=0.1)
+            e = tiles[("e", u)]
+            nc.scalar.activation(out=e[:, RV:], in_=e[:, RV:], func=ACT.Relu, scale=0.1)
+            nc.vector.tensor_scalar(
+                out=e[:, 0:RV], in0=e[:, 0:RV], scalar1=0.1, scalar2=0.0, op0=ALU.mult, op1=ALU.max
+            )
 
         def ph_out(u):
             for v, n in runs(u):
                 gi, j = unit_group[v]
+                if j == 0:
+                    o = epi.tile([P, GROUPS[gi] * D], F32, name="o", bufs=3)
+                    tiles[("o", gi)] = o
                 nc.vector.scalar_tensor_tensor(
-                    out=e_slice(v, n), in0=tiles[("rn", gi)][:, D * j : D * (j + n)], scalar=0.9, in1=e_slice(v, n),
-                    op0=ALU.mult, op1=ALU.add,
+                    out=tiles[("o", gi)][:, D * j : D * (j + n)],
+                    in0=tiles[("rn", gi)][:, D * j : D * (j + n)],
+                    scalar=0.9,
+                    in1=e_slice(v, n),
+                    op0=ALU.mult,
+                    op1=ALU.add,
                 )
                 if j + n == GROUPS[gi]:
-                    nc.sync.dma_start(out=gview(out, gi), in_=tiles[("e", gi)][:])
+                    nc.sync.dma_start(out=gview(out, gi), in_=tiles[("o", gi)][:])
 
         load(0, "x")
         load(0, "som")
-        load(0, "pr")
         load_w1(0)
         load_w1(1)
+        load(0, "pr")
         load(1, "x")
         load(1, "som")
+        load_w3()
+        load_w2()
         load(1, "pr")
         load(2, "x")
         load(2, "som")
         load(2, "pr")
-        load_w3()
-        load_w2()
-        head_loads = {(0, "x"), (0, "som"), (0, "pr"), (1, "x"), (1, "som"), (1, "pr"), (2, "x"), (2, "som"), (2, "pr")}
+        head_loads = [(gi, which) for gi in range(3) for which in ("x", "som", "pr")]
         loads_at = {}
         for gi in range(len(GROUPS)):
             for which in ("x", "som", "pr", "rn"):
@@ -284,56 +290,57 @@ def tile_pecircuits_pb_t_kernel(
                 load(gi, which)
             if ok(k - O_TC):
                 ph_tc(k - O_TC)
-            if ok(k - O_C):
-                ph_c(k - O_C)
             if ok(k - O_D):
                 ph_d(k - O_D)
+            if ok(k - O_C):
+                ph_c(k - O_C)
             if k % 2 == 0:
                 for u in (k, k + 1):
                     if ok(u):
                         ph_t(u)
-            if ok(k - O_R):
-                ph_r(k - O_R)
-            if ok(k - O_RELU):
-                ph_relu(k - O_RELU)
             if ok(k - O_Q):
                 ph_q(k - O_Q)
+            if k % 2 == 0 and ok(k - O_B):
+                ph_b(k - O_B)
+            if k % 2 == 1 and ok(k - O_OUT):
+                ph_relu(k - O_OUT)
+            if ok(k - O_R):
+                ph_r(k - O_R)
             if ok(k - O_QR):
                 ph_qr(k - O_QR)
-            if ok(k - O_B):
-                ph_b(k - O_B)
-            if ok(k - O_OUT):
+            if k % 2 == 1 and ok(k - O_OUT):
                 ph_out(k - O_OUT)
-            if ok(k - O_A):
-                ph_a(k - O_A)
+            if 0 <= k - 3 < 2 * E_PAIRS:
+                ph_a(k - 3, nc.vector)
+            if k % 2 == 0 and 2 * E_PAIRS <= k - O_AV < NU:
+                ph_a(k - O_AV, nc.vector)
+            if k % 2 == 1 and 2 * E_PAIRS <= k - O_AG < NU:
+                ph_a(k - O_AG + 1, nc.gpsimd)
+            if k == 0:
+                for q in range(2):
+                    w_t("w1", q, 0)
+                    w_t("w1", q, 1)
+                for q in range(2):
+                    w_c("w1", q, 0, True)
+                    w_c("w1", q, 1, False)
+                    w_q("w1", q)
             if k == 1:
-                w_t("w1", 0, 0)
-                w_t("w1", 0, 1)
-                w_t("w1", 1, 0)
-                w_t("w1", 1, 1)
-                w_c("w1", 0, 0, True)
-                w_c("w1", 0, 1, False)
-                w_q("w1", 0)
-                w_c("w1", 1, 0, True)
-                w_c("w1", 1, 1, False)
-                w_q("w1", 1)
-            if k == 4:
                 w_t("w3", 0, 0)
                 w_t("w3", 0, 1)
-            if k == 5:
+            if k == 2:
                 w_c("w3", 0, 0, True)
                 w_c("w3", 0, 1, False)
                 w_t("w2", 0, 0)
                 w_t("w2", 0, 1)
-            if k == 6:
+            if k == 3:
                 w_q("w3", 0)
                 w_c("w2", 0, 0, True)
                 w_c("w2", 0, 1, False)
                 w_t("w2", 1, 0)
                 w_t("w2", 1, 1)
-            if k == 7:
+            if k == 4:
                 w_q("w2", 0)
                 w_c("w2", 1, 0, True)
                 w_c("w2", 1, 1, False)
-            if k == 8:
+            if k == 5:
                 w_q("w2", 1)

@@ -15,16 +15,16 @@ P = 128
 B, D, NP, NS = 4096, 512, 1024, 512
 FLOPS = 2 * B * (D * NP + NP * D + NS * D)
 NU = B // P
-GROUPS = (2, 2, 2, 2, 4, 4, 4, 4, 4, 2, 1, 1)
-O_TC, O_Q, O_C, O_R, O_QR, O_D, O_B, O_OUT = 1, 2, 4, 5, 6, 7, 8, 9
-E_PAIRS = 3
-O_AG = O_OUT - 2 * E_PAIRS
-O_AV = O_AG + 1
-RV = 256
-LEAD = 4
+GROUPS = (1, 1, 2, 2, 2, 4, 4, 4, 4, 4, 2, 1, 1)
+E_PAIRS = 4
+LEAD = 3
+AV = 640
+RV = 192
+GB = 6
+O_D, O_Q, O_QR, O_OUT = 7, 3, 6, 9
 NBUF = {"x": 4, "som": 4, "pr": 4, "rn": 4}
-LAST_USE = {"x": 5, "som": 0, "pr": 5, "rn": O_OUT}
-FIRST_USE = {"x": 0, "som": 0, "pr": 0, "rn": O_OUT - 4}
+LAST_USE = {"x": 4, "som": 0, "pr": 4, "rn": O_OUT}
+FIRST_USE = {"x": 0, "som": 0, "pr": 1, "rn": O_OUT - 4}
 
 
 def tile_pecircuits_pb_t_kernel(
@@ -40,7 +40,7 @@ def tile_pecircuits_pb_t_kernel(
     with ExitStack() as ctx:
         const = ctx.enter_context(tc.tile_pool(name="const", bufs=1))
         inp = ctx.enter_context(tc.tile_pool(name="inp", bufs=4))
-        grp = ctx.enter_context(tc.tile_pool(name="grp", bufs=3))
+        grp = ctx.enter_context(tc.tile_pool(name="grp", bufs=GB))
         cod = ctx.enter_context(tc.tile_pool(name="cod", bufs=3))
         epi = ctx.enter_context(tc.tile_pool(name="epi", bufs=6))
         ps_t = ctx.enter_context(tc.psum_pool(name="ps_t", bufs=2))
@@ -96,10 +96,10 @@ def tile_pecircuits_pb_t_kernel(
         w2s = const.tile([P, 1024], U8, align_bytes=64)
         w3s = const.tile([P, 512], U8, align_bytes=64)
 
-        def load_w1(g):
+        def load_w1(i, n):
             nc.sync.dma_start(
-                out=w1_sb[:, 2048 * g : 2048 * g + 2048].rearrange("p (a r) -> p a r", a=2),
-                in_=W_pv1_ff[512 * g : 512 * g + 512, :].rearrange("(a p e) k -> p a (e k)", a=2, p=P, e=2),
+                out=w1_sb[:, 1024 * i : 1024 * (i + n)].rearrange("p (a r) -> p a r", a=n),
+                in_=W_pv1_ff[256 * i : 256 * (i + n), :].rearrange("(a p e) k -> p a (e k)", a=n, p=P, e=2),
             )
 
         def load_w2():
@@ -161,15 +161,24 @@ def tile_pecircuits_pb_t_kernel(
             tiles[("cxs", u)] = codes
             tiles[("sxs", u)] = scales
 
-        def ph_a(u, engine):
-            if ("e", u - u % 2) not in tiles:
+        def ph_a(u, c0, c1, engine):
+            if ("e", u) not in tiles:
                 e = epi.tile([P, 2 * D], F32, name="e", bufs=E_PAIRS)
-                tiles[("e", u - u % 2)] = e
-            gi, j = unit_group[u]
-            cols = slice(D * j, D * j + D)
-            engine.tensor_tensor(
-                out=e_slice(u), in0=tiles[("pr", gi)][:, cols], in1=tiles[("x", gi)][:, cols], op=ALU.subtract
-            )
+                tiles[("e", u)] = e
+            for v, a, b in ((u, c0, min(c1, D)), (u + 1, max(c0, D) - D, c1 - D)):
+                if a < b and not (v == u + 1 and c0 < D and unit_group[u][0] == unit_group[u + 1][0]):
+                    gi, j = unit_group[v]
+                    n = b - a
+                    if v == u and c1 > D and unit_group[u][0] == unit_group[u + 1][0]:
+                        n = c1 - a
+                    ea = a + D * (v - u)
+                    cols = slice(D * j + a, D * j + a + n)
+                    engine.tensor_tensor(
+                        out=tiles[("e", u)][:, ea : ea + n],
+                        in0=tiles[("pr", gi)][:, cols],
+                        in1=tiles[("x", gi)][:, cols],
+                        op=ALU.subtract,
+                    )
 
         def ph_c(u):
             xc, xs = tiles[("cxs", u)], tiles[("sxs", u)]
@@ -235,8 +244,8 @@ def tile_pecircuits_pb_t_kernel(
 
         def ph_relu(u):
             e = tiles[("e", u)]
-            nc.scalar.activation(out=e[:, RV:], in_=e[:, RV:], func=ACT.Relu, scale=0.1)
-            nc.vector.tensor_scalar(
+            if RV < 1024: nc.scalar.activation(out=e[:, RV:], in_=e[:, RV:], func=ACT.Relu, scale=0.1)
+            if RV: nc.vector.tensor_scalar(
                 out=e[:, 0:RV], in0=e[:, 0:RV], scalar1=0.1, scalar2=0.0, op0=ALU.mult, op1=ALU.max
             )
 
@@ -259,18 +268,20 @@ def tile_pecircuits_pb_t_kernel(
 
         load(0, "x")
         load(0, "som")
-        load_w1(0)
-        load_w1(1)
-        load(0, "pr")
         load(1, "x")
         load(1, "som")
+        load_w1(0, 1)
+        load_w1(1, 1)
+        load_w1(2, 1)
+        load_w1(3, 1)
         load_w3()
+        load(0, "pr")
         load_w2()
         load(1, "pr")
         load(2, "x")
         load(2, "som")
         load(2, "pr")
-        head_loads = [(gi, which) for gi in range(3) for which in ("x", "som", "pr")]
+        head_loads = [(0, 'x'), (0, 'som'), (1, 'x'), (1, 'som'), (0, 'pr'), (1, 'pr'), (2, 'x'), (2, 'som'), (2, 'pr')]
         loads_at = {}
         for gi in range(len(GROUPS)):
             for which in ("x", "som", "pr", "rn"):
@@ -285,61 +296,65 @@ def tile_pecircuits_pb_t_kernel(
                     loads_at[k] = []
                 loads_at[k].append((gi, which))
 
-        for k in range(0, NU + O_OUT):
+        for k in range(0, NU + 11):
             for gi, which in loads_at.get(k, []):
                 load(gi, which)
-            if ok(k - O_TC):
-                ph_tc(k - O_TC)
-            if ok(k - O_D):
-                ph_d(k - O_D)
-            if ok(k - O_C):
-                ph_c(k - O_C)
+            if ok(k - 1):
+                ph_tc(k - 1)
+            if ok(k - 7):
+                ph_d(k - 7)
             if k % 2 == 0:
                 for u in (k, k + 1):
                     if ok(u):
                         ph_t(u)
-            if ok(k - O_Q):
-                ph_q(k - O_Q)
-            if k % 2 == 0 and ok(k - O_B):
-                ph_b(k - O_B)
-            if k % 2 == 1 and ok(k - O_OUT):
-                ph_relu(k - O_OUT)
-            if ok(k - O_R):
-                ph_r(k - O_R)
-            if ok(k - O_QR):
-                ph_qr(k - O_QR)
-            if k % 2 == 1 and ok(k - O_OUT):
-                ph_out(k - O_OUT)
-            if 0 <= k - 3 < 2 * E_PAIRS:
-                ph_a(k - 3, nc.vector)
-            if k % 2 == 0 and 2 * E_PAIRS <= k - O_AV < NU:
-                ph_a(k - O_AV, nc.vector)
-            if k % 2 == 1 and 2 * E_PAIRS <= k - O_AG < NU:
-                ph_a(k - O_AG + 1, nc.gpsimd)
+            if ok(k - 4):
+                ph_c(k - 4)
+            if (k - 9) % 2 == 0 and ok(k - 9):
+                ph_relu(k - 9)
+            if ok(k - 5):
+                ph_r(k - 5)
+            if ok(k - 3):
+                ph_q(k - 3)
+            if (k - 8) % 2 == 0 and ok(k - 8):
+                ph_b(k - 8)
+            if ok(k - 6):
+                ph_qr(k - 6)
+            if (k - 9) % 2 == 0 and ok(k - 9):
+                ph_out(k - 9)
+            if 0 <= k - 1 < 2 * E_PAIRS:
+                u = k - 1
+                ph_a(u // 2 * 2, D * (u % 2), D * (u % 2) + D, nc.vector)
+            if AV < 2 * D and (k - 1) % 2 == 0 and 2 * E_PAIRS <= k - 1 < NU:
+                ph_a(k - 1, AV, 2 * D, nc.gpsimd)
+            if (k - 2) % 2 == 0 and 2 * E_PAIRS <= k - 2 < NU:
+                ph_a(k - 2, 0, AV, nc.vector)
             if k == 0:
-                for q in range(2):
-                    w_t("w1", q, 0)
-                    w_t("w1", q, 1)
-                for q in range(2):
-                    w_c("w1", q, 0, True)
-                    w_c("w1", q, 1, False)
-                    w_q("w1", q)
-            if k == 1:
+                w_t("w1", 0, 0)
+                w_t("w1", 0, 1)
+                w_t("w1", 1, 0)
+                w_t("w1", 1, 1)
+                w_c("w1", 0, 0, True)
+                w_c("w1", 0, 1, False)
+                w_q("w1", 0)
+                w_c("w1", 1, 0, True)
+                w_c("w1", 1, 1, False)
+                w_q("w1", 1)
                 w_t("w3", 0, 0)
                 w_t("w3", 0, 1)
-            if k == 2:
                 w_c("w3", 0, 0, True)
                 w_c("w3", 0, 1, False)
+            if k == 1:
+                w_q("w3", 0)
                 w_t("w2", 0, 0)
                 w_t("w2", 0, 1)
-            if k == 3:
-                w_q("w3", 0)
+            if k == 2:
                 w_c("w2", 0, 0, True)
                 w_c("w2", 0, 1, False)
+            if k == 3:
+                w_q("w2", 0)
                 w_t("w2", 1, 0)
                 w_t("w2", 1, 1)
             if k == 4:
-                w_q("w2", 0)
                 w_c("w2", 1, 0, True)
                 w_c("w2", 1, 1, False)
             if k == 5:

@@ -243,14 +243,18 @@ def tile_pecircuits_pb_t_kernel(
                 nc.vector.tensor_tensor(out=e_slice(v), in0=e_slice(v), in1=tiles[("acc", v)][:], op=ALU.subtract)
 
         def ph_relu(u):
+            if u == NU - 2:
+                for v in (u, u + 1):
+                    nc.scalar.activation(out=e_slice(v), in_=e_slice(v), func=ACT.Relu, scale=0.1)
+                return
             e = tiles[("e", u)]
             if RV < 1024: nc.scalar.activation(out=e[:, RV:], in_=e[:, RV:], func=ACT.Relu, scale=0.1)
             if RV: nc.vector.tensor_scalar(
                 out=e[:, 0:RV], in0=e[:, 0:RV], scalar1=0.1, scalar2=0.0, op0=ALU.mult, op1=ALU.max
             )
 
-        def ph_out(u):
-            for v, n in runs(u):
+        def ph_out(spans):
+            for v, n in spans:
                 gi, j = unit_group[v]
                 if j == 0:
                     o = epi.tile([P, GROUPS[gi] * D], F32, name="o", bufs=3)
@@ -320,7 +324,9 @@ def tile_pecircuits_pb_t_kernel(
             if ok(k - 6):
                 ph_qr(k - 6)
             if (k - 9) % 2 == 0 and ok(k - 9):
-                ph_out(k - 9)
+                ph_out(((k - 9, 1),) if k - 9 == NU - 4 else runs(k - 9))
+            if k - 10 == NU - 4:
+                ph_out(((NU - 3, 1),))
             if 0 <= k - 1 < 2 * E_PAIRS:
                 u = k - 1
                 ph_a(u // 2 * 2, D * (u % 2), D * (u % 2) + D, nc.vector)

@@ -104,14 +104,14 @@ def tile_pecircuits_pb_t_kernel(
 
         def load_w2():
             nc.sync.dma_start(
-                out=w2_sb[:].rearrange("p (a r) -> p a r", a=4),
-                in_=W_inh_pe_neg.rearrange("(a p) k -> p a k", p=P),
+                out=w2_sb[:],
+                in_=W_inh_pe_neg.rearrange("(p n) k -> p (n k)", n=4),
             )
 
         def load_w3():
             nc.sync.dma_start(
-                out=w3_sb[:].rearrange("p (a r) -> p a r", a=4),
-                in_=W_som_dend.rearrange("(a p) k -> p a k", p=P),
+                out=w3_sb[:],
+                in_=W_som_dend.rearrange("(p n) k -> p (n k)", n=4),
             )
 
         weights = {
@@ -240,7 +240,9 @@ def tile_pecircuits_pb_t_kernel(
 
         def ph_b(u):
             for v in (u, u + 1):
-                nc.vector.tensor_tensor(out=e_slice(v), in0=e_slice(v), in1=tiles[("acc", v)][:], op=ALU.subtract)
+                e = e_slice(v).rearrange("m (p n) -> m p n", n=4)
+                acc = tiles[("acc", v)][:].rearrange("m (n p) -> m p n", n=4)
+                nc.vector.tensor_tensor(out=e, in0=e, in1=acc, op=ALU.subtract)
 
         def ph_relu(u):
             if u == NU - 2:

@@ -18,8 +18,10 @@ NU = B // P
 GROUPS = (1, 1, 2, 2, 2, 4, 4, 4, 4, 4, 2, 1, 1)
 E_PAIRS = 4
 LEAD = 3
-AV = 640
-RV = 192
+AV = 608
+RV = 160
+RV_LATE = 512
+LATE = NU - 6
 GB = 6
 O_D, O_Q, O_QR, O_OUT = 7, 3, 6, 9
 NBUF = {"x": 4, "som": 4, "pr": 4, "rn": 4}
@@ -250,10 +252,9 @@ def tile_pecircuits_pb_t_kernel(
                     nc.scalar.activation(out=e_slice(v), in_=e_slice(v), func=ACT.Relu, scale=0.1)
                 return
             e = tiles[("e", u)]
-            if RV < 1024: nc.scalar.activation(out=e[:, RV:], in_=e[:, RV:], func=ACT.Relu, scale=0.1)
-            if RV: nc.vector.tensor_scalar(
-                out=e[:, 0:RV], in0=e[:, 0:RV], scalar1=0.1, scalar2=0.0, op0=ALU.mult, op1=ALU.max
-            )
+            w = RV_LATE if u >= LATE else RV
+            nc.scalar.activation(out=e[:, w:], in_=e[:, w:], func=ACT.Relu, scale=0.1)
+            nc.vector.tensor_scalar(out=e[:, 0:w], in0=e[:, 0:w], scalar1=0.1, scalar2=0.0, op0=ALU.mult, op1=ALU.max)
 
         def ph_out(spans):
             for v, n in spans:
@@ -261,15 +262,22 @@ def tile_pecircuits_pb_t_kernel(
                 if j == 0:
                     o = epi.tile([P, GROUPS[gi] * D], F32, name="o", bufs=3)
                     tiles[("o", gi)] = o
-                nc.vector.scalar_tensor_tensor(
-                    out=tiles[("o", gi)][:, D * j : D * (j + n)],
-                    in0=tiles[("rn", gi)][:, D * j : D * (j + n)],
-                    scalar=0.9,
-                    in1=e_slice(v, n),
-                    op0=ALU.mult,
-                    op1=ALU.add,
-                )
-                if j + n == GROUPS[gi]:
+                parts = 2 if v == NU - 1 else 1
+                w = D * n // parts
+                for c in range(D * j, D * (j + n), w):
+                    o_cols = slice(c, c + w)
+                    e_cols = slice(c - D * j, c - D * j + w)
+                    nc.vector.scalar_tensor_tensor(
+                        out=tiles[("o", gi)][:, o_cols],
+                        in0=tiles[("rn", gi)][:, o_cols],
+                        scalar=0.9,
+                        in1=e_slice(v, n)[:, e_cols],
+                        op0=ALU.mult,
+                        op1=ALU.add,
+                    )
+                    if parts == 2:
+                        nc.sync.dma_start(out=gview(out, gi)[:, o_cols], in_=tiles[("o", gi)][:, o_cols])
+                if j + n == GROUPS[gi] and parts == 1:
                     nc.sync.dma_start(out=gview(out, gi), in_=tiles[("o", gi)][:])
 
         load(0, "x")

@@ -17,14 +17,14 @@ FLOPS = 2 * B * (D * NP + NP * D + NS * D)
 NU = B // P
 GROUPS = (1, 1, 2, 2, 2, 4, 4, 4, 4, 4, 2, 1, 1)
 E_PAIRS = 4
-LEAD = 3
+LEAD = 4
 AV = 608
 RV = 160
 RV_LATE = 512
 LATE = NU - 6
 GB = 6
 O_D, O_Q, O_QR, O_OUT = 7, 3, 6, 9
-NBUF = {"x": 4, "som": 4, "pr": 4, "rn": 4}
+NBUF = {"x": 5, "som": 5, "pr": 5, "rn": 4}
 LAST_USE = {"x": 4, "som": 0, "pr": 4, "rn": O_OUT}
 FIRST_USE = {"x": 0, "som": 0, "pr": 1, "rn": O_OUT - 4}
 

@@ -15,16 +15,16 @@ P = 128
 B, D, NP, NS = 4096, 512, 1024, 512
 FLOPS = 2 * B * (D * NP + NP * D + NS * D)
 NU = B // P
-GROUPS = (1, 1, 2, 2, 2, 4, 4, 4, 4, 4, 2, 1, 1)
-E_PAIRS = 4
-LEAD = 4
-AV = 608
-RV = 160
 RV_LATE = 512
 LATE = NU - 6
+GROUPS = (1, 1, 2, 2, 2, 4, 4, 4, 4, 4, 2, 1, 1)
+E_PAIRS = 3
+LEAD = 4
+AV = 640
+RV = 128
 GB = 6
-O_D, O_Q, O_QR, O_OUT = 7, 3, 6, 9
-NBUF = {"x": 5, "som": 5, "pr": 5, "rn": 4}
+O_D, O_Q, O_QR, O_OUT = 5, 1, 4, 7
+NBUF = {"x": 4, "som": 4, "pr": 4, "rn": 4}
 LAST_USE = {"x": 4, "som": 0, "pr": 4, "rn": O_OUT}
 FIRST_USE = {"x": 0, "som": 0, "pr": 1, "rn": O_OUT - 4}
 
@@ -260,42 +260,33 @@ def tile_pecircuits_pb_t_kernel(
             for v, n in spans:
                 gi, j = unit_group[v]
                 if j == 0:
-                    o = epi.tile([P, GROUPS[gi] * D], F32, name="o", bufs=3)
+                    o = epi.tile([P, GROUPS[gi] * D], F32, name="o", bufs=4)
                     tiles[("o", gi)] = o
-                parts = 2 if v == NU - 1 else 1
-                w = D * n // parts
-                for c in range(D * j, D * (j + n), w):
-                    o_cols = slice(c, c + w)
-                    e_cols = slice(c - D * j, c - D * j + w)
-                    nc.vector.scalar_tensor_tensor(
-                        out=tiles[("o", gi)][:, o_cols],
-                        in0=tiles[("rn", gi)][:, o_cols],
-                        scalar=0.9,
-                        in1=e_slice(v, n)[:, e_cols],
-                        op0=ALU.mult,
-                        op1=ALU.add,
-                    )
-                    if parts == 2:
-                        nc.sync.dma_start(out=gview(out, gi)[:, o_cols], in_=tiles[("o", gi)][:, o_cols])
-                if j + n == GROUPS[gi] and parts == 1:
+                nc.vector.scalar_tensor_tensor(
+                    out=tiles[("o", gi)][:, D * j : D * (j + n)],
+                    in0=tiles[("rn", gi)][:, D * j : D * (j + n)],
+                    scalar=0.9,
+                    in1=e_slice(v, n),
+                    op0=ALU.mult,
+                    op1=ALU.add,
+                )
+                if j + n == GROUPS[gi]:
                     nc.sync.dma_start(out=gview(out, gi), in_=tiles[("o", gi)][:])
 
         load(0, "x")
         load(0, "som")
         load(1, "x")
         load(1, "som")
-        load_w1(0, 1)
-        load_w1(1, 1)
-        load_w1(2, 1)
-        load_w1(3, 1)
         load_w3()
-        load(0, "pr")
+        load_w1(0, 2)
+        load_w1(2, 2)
         load_w2()
-        load(1, "pr")
+        load(0, "pr")
         load(2, "x")
         load(2, "som")
+        load(1, "pr")
         load(2, "pr")
-        head_loads = [(0, 'x'), (0, 'som'), (1, 'x'), (1, 'som'), (0, 'pr'), (1, 'pr'), (2, 'x'), (2, 'som'), (2, 'pr')]
+        head_loads = [(0, 'x'), (0, 'som'), (1, 'x'), (1, 'som'), (0, 'pr'), (2, 'x'), (2, 'som'), (1, 'pr'), (2, 'pr')]
         loads_at = {}
         for gi in range(len(GROUPS)):
             for which in ("x", "som", "pr", "rn"):
@@ -310,41 +301,46 @@ def tile_pecircuits_pb_t_kernel(
                     loads_at[k] = []
                 loads_at[k].append((gi, which))
 
-        for k in range(0, NU + 11):
+        for k in range(0, NU + 9):
             for gi, which in loads_at.get(k, []):
                 load(gi, which)
             if ok(k - 1):
                 ph_tc(k - 1)
-            if ok(k - 7):
-                ph_d(k - 7)
+            if ok(k - 5):
+                ph_d(k - 5)
+            if ok(k - 2):
+                ph_c(k - 2)
             if k % 2 == 0:
                 for u in (k, k + 1):
                     if ok(u):
                         ph_t(u)
-            if ok(k - 4):
-                ph_c(k - 4)
-            if (k - 9) % 2 == 0 and ok(k - 9):
-                ph_relu(k - 9)
-            if ok(k - 5):
-                ph_r(k - 5)
+            if (k - 7) % 2 == 0 and ok(k - 7):
+                ph_relu(k - 7)
             if ok(k - 3):
-                ph_q(k - 3)
-            if (k - 8) % 2 == 0 and ok(k - 8):
-                ph_b(k - 8)
-            if ok(k - 6):
-                ph_qr(k - 6)
-            if (k - 9) % 2 == 0 and ok(k - 9):
-                ph_out(((k - 9, 1),) if k - 9 == NU - 4 else runs(k - 9))
-            if k - 10 == NU - 4:
-                ph_out(((NU - 3, 1),))
-            if 0 <= k - 1 < 2 * E_PAIRS:
-                u = k - 1
+                ph_r(k - 3)
+            if ok(k - 4):
+                ph_qr(k - 4)
+            if (k - 6) % 2 == 0 and ok(k - 6):
+                ph_b(k - 6)
+            if ok(k - 1):
+                ph_q(k - 1)
+            if 0 <= k - 2 < 2 * E_PAIRS:
+                u = k - 2
                 ph_a(u // 2 * 2, D * (u % 2), D * (u % 2) + D, nc.vector)
+            if (k - 7) % 2 == 0 and ok(k - 7):
+                ph_out(((k - 7, 1),) if k - 7 == NU - 4 else runs(k - 7))
+            if k - 8 == NU - 4:
+                ph_out(((NU - 3, 1),))
             if AV < 2 * D and (k - 1) % 2 == 0 and 2 * E_PAIRS <= k - 1 < NU:
                 ph_a(k - 1, AV, 2 * D, nc.gpsimd)
             if (k - 2) % 2 == 0 and 2 * E_PAIRS <= k - 2 < NU:
                 ph_a(k - 2, 0, AV, nc.vector)
             if k == 0:
+                w_t("w3", 0, 0)
+                w_t("w3", 0, 1)
+                w_c("w3", 0, 0, True)
+                w_c("w3", 0, 1, False)
+            if k == 1:
                 w_t("w1", 0, 0)
                 w_t("w1", 0, 1)
                 w_t("w1", 1, 0)
@@ -355,23 +351,16 @@ def tile_pecircuits_pb_t_kernel(
                 w_c("w1", 1, 0, True)
                 w_c("w1", 1, 1, False)
                 w_q("w1", 1)
-                w_t("w3", 0, 0)
-                w_t("w3", 0, 1)
-                w_c("w3", 0, 0, True)
-                w_c("w3", 0, 1, False)
-            if k == 1:
                 w_q("w3", 0)
                 w_t("w2", 0, 0)
                 w_t("w2", 0, 1)
             if k == 2:
                 w_c("w2", 0, 0, True)
                 w_c("w2", 0, 1, False)
-            if k == 3:
                 w_q("w2", 0)
                 w_t("w2", 1, 0)
                 w_t("w2", 1, 1)
-            if k == 4:
+            if k == 3:
                 w_c("w2", 1, 0, True)
                 w_c("w2", 1, 1, False)
-            if k == 5:
                 w_q("w2", 1)

from contextlib import ExitStack

import concourse.mybir as mybir
from concourse.masks import make_identity

F32 = mybir.dt.float32
BF16 = mybir.dt.bfloat16
U32 = mybir.dt.uint32
U8 = mybir.dt.uint8
FP8X4 = mybir.dt.float8_e4m3fn_x4
ALU = mybir.AluOpType
ACT = mybir.ActivationFunctionType

P = 128
B, D, NP, NS = 4096, 512, 1024, 512
FLOPS = 2 * B * (D * NP + NP * D + NS * D)
NU = B // P
RV_LATE = 512
LATE = NU - 6
GROUPS = (1, 1, 2, 2, 2, 4, 4, 4, 4, 4, 2, 1, 1)
E_PAIRS = 3
LEAD = 4
AV = 640
RV = 128
GB = 6
O_D, O_Q, O_QR, O_OUT = 5, 1, 4, 7
NBUF = {"x": 4, "som": 4, "pr": 4, "rn": 4}
LAST_USE = {"x": 4, "som": 0, "pr": 4, "rn": O_OUT}
FIRST_USE = {"x": 0, "som": 0, "pr": 1, "rn": O_OUT - 4}


def tile_pecircuits_pb_t_kernel(
    tc, x_batch, predicted, r_som, r_neg_batch, W_pv1_ff, W_inh_pe_neg, W_som_dend, out
):
    nc = tc.nc
    first = [sum(GROUPS[:i]) for i in range(len(GROUPS))]
    unit_group = {}
    for gi, t in enumerate(GROUPS):
        for j in range(t):
            unit_group[first[gi] + j] = (gi, j)

    with ExitStack() as ctx:
        const = ctx.enter_context(tc.tile_pool(name="const", bufs=1))
        inp = ctx.enter_context(tc.tile_pool(name="inp", bufs=4))
        grp = ctx.enter_context(tc.tile_pool(name="grp", bufs=GB))
        cod = ctx.enter_context(tc.tile_pool(name="cod", bufs=3))
        epi = ctx.enter_context(tc.tile_pool(name="epi", bufs=6))
        ps_t = ctx.enter_context(tc.psum_pool(name="ps_t", bufs=2))
        ps_c = ctx.enter_context(tc.psum_pool(name="ps_c", bufs=4))
        ps_d = ctx.enter_context(tc.psum_pool(name="ps_d", bufs=2))

        ident = const.tile([P, P], F32)
        make_identity(nc, ident[:])
        ctx.enter_context(tc.manual_schedule())

        def gview(ap, gi):
            t = GROUPS[gi]
            r0 = P * first[gi]
            return ap[r0 : r0 + P * t, :].rearrange("(p t) d -> p (t d)", t=t)

        srcs = {"x": x_batch, "som": r_som, "pr": predicted, "rn": r_neg_batch}
        tiles = {}

        def load(gi, which):
            t = inp.tile([P, GROUPS[gi] * D], BF16, name="in_" + which, bufs=NBUF[which])
            nc.sync.dma_start(out=t[:], in_=gview(srcs[which], gi))
            tiles[(which, gi)] = t

        def t_bank(pool, tag, blocks):
            bank = pool.tile([P, 2, 2, P], F32, name=tag, tag=tag)
            for l, (src32, off) in enumerate(blocks):
                for u in range(2):
                    o = off + P * u
                    nc.tensor.transpose(bank[:, l, u, :], src32[:, o : o + P], ident[:])
            return bank

        def t_copy(bank, dst32, on_vector):
            dst = dst32.rearrange("p (l j u) -> p l j u", l=2, u=2)
            src = bank[:].rearrange("p l u j -> p l j u")
            if on_vector:
                nc.vector.tensor_copy(out=dst, in_=src)
            else:
                nc.scalar.copy(out=dst, in_=src)

        def quantise(codes, scales, grouped):
            nc.vector.quantize_mx(out=codes.bitcast(FP8X4), scales=scales, in_=grouped)

        w1_sb = const.tile([P, 4096], BF16)
        w2_sb = const.tile([P, 4096], BF16)
        w3_sb = const.tile([P, 2048], BF16)
        w1g = const.tile([P, 4096], BF16, align_bytes=64)
        w2g = const.tile([P, 4096], BF16, align_bytes=64)
        w3g = const.tile([P, 2048], BF16, align_bytes=64)
        w1c = const.tile([P, 1024], U32, align_bytes=64)
        w2c = const.tile([P, 1024], U32, align_bytes=64)
        w3c = const.tile([P, 512], U32, align_bytes=64)
        w1s = const.tile([P, 1024], U8, align_bytes=64)
        w2s = const.tile([P, 1024], U8, align_bytes=64)
        w3s = const.tile([P, 512], U8, align_bytes=64)

        def load_w1(i, n):
            nc.sync.dma_start(
                out=w1_sb[:, 1024 * i : 1024 * (i + n)].rearrange("p (a r) -> p a r", a=n),
                in_=W_pv1_ff[256 * i : 256 * (i + n), :].rearrange("(a p e) k -> p a (e k)", a=n, p=P, e=2),
            )

        def load_w2():
            nc.sync.dma_start(
                out=w2_sb[:],
                in_=W_inh_pe_neg.rearrange("(p n) k -> p (n k)", n=4),
            )

        def load_w3():
            nc.sync.dma_start(
                out=w3_sb[:],
                in_=W_som_dend.rearrange("(p n) k -> p (n k)", n=4),
            )

        weights = {
            "w1": (ps_c, "cb", w1_sb, w1g, w1c, w1s, lambda q: [1024 * q + 256 * n for n in range(4)]),
            "w2": (ps_d, "db", w2_sb, w2g, w2c, w2s, lambda q: [512 * n + 256 * q for n in range(4)]),
            "w3": (ps_d, "db", w3_sb, w3g, w3c, w3s, lambda q: [256 * n for n in range(4)]),
        }

        def w_t(key, q, h):
            pool, tag, src, grouped, codes, scales, offs_of = weights[key]
            s32 = src[:].bitcast(F32)
            offs = offs_of(q)
            tiles[("wb", key, q, h)] = t_bank(pool, tag, [(s32, offs[2 * h]), (s32, offs[2 * h + 1])])

        def w_c(key, q, h, on_vector):
            grouped = weights[key][3]
            o = 1024 * q + 512 * h
            t_copy(tiles[("wb", key, q, h)], grouped[:].bitcast(F32)[:, o : o + 512], on_vector)

        def w_q(key, q):
            pool, tag, src, grouped, codes, scales, offs_of = weights[key]
            quantise(
                codes[:, 512 * q : 512 * q + 512],
                scales[:, 512 * q : 512 * q + 512],
                grouped[:, 2048 * q : 2048 * q + 2048],
            )

        def ok(u):
            return 0 <= u < NU

        def ph_t(u):
            gi, j = unit_group[u]
            tiles[("tb", u)] = t_bank(
                ps_t, "tb",
                [(tiles[("x", gi)][:].bitcast(F32), 256 * j), (tiles[("som", gi)][:].bitcast(F32), 256 * j)],
            )

        def ph_tc(u):
            g = grp.tile([P, 1024], BF16, name="g_xs", align_bytes=64)
            t_copy(tiles[("tb", u)], g[:].bitcast(F32), False)
            tiles[("gxs", u)] = g

        def ph_q(u):
            codes = cod.tile([P, 256], U32, name="c_xs", align_bytes=64, bufs=O_D - O_Q + 2)
            scales = cod.tile([P, 256], U8, name="s_xs", align_bytes=64, bufs=O_D - O_Q + 2)
            quantise(codes[:], scales[:], tiles[("gxs", u)][:])
            tiles[("cxs", u)] = codes
            tiles[("sxs", u)] = scales

        def ph_a(u, c0, c1, engine):
            if ("e", u) not in tiles:
                e = epi.tile([P, 2 * D], F32, name="e", bufs=E_PAIRS)
                tiles[("e", u)] = e
            for v, a, b in ((u, c0, min(c1, D)), (u + 1, max(c0, D) - D, c1 - D)):
                if a < b and not (v == u + 1 and c0 < D and unit_group[u][0] == unit_group[u + 1][0]):
                    gi, j = unit_group[v]
                    n = b - a
                    if v == u and c1 > D and unit_group[u][0] == unit_group[u + 1][0]:
                        n = c1 - a
                    ea = a + D * (v - u)
                    cols = slice(D * j + a, D * j + a + n)
                    engine.tensor_tensor(
                        out=tiles[("e", u)][:, ea : ea + n],
                        in0=tiles[("pr", gi)][:, cols],
                        in1=tiles[("x", gi)][:, cols],
                        op=ALU.subtract,
                    )

        def ph_c(u):
            xc, xs = tiles[("cxs", u)], tiles[("sxs", u)]
            for g in range(2):
                bank = ps_c.tile([P, 4, P], F32, name="cb", tag="cb")
                for t in range(4):
                    m = P * (4 * g + t)
                    nc.tensor.matmul_mx(
                        out=bank[:, t, :],
                        lhsT=w1c[:, m : m + P].bitcast(FP8X4),
                        lhsT_scale=w1s[:, m : m + P],
                        rhs=xc[:, 0:P].bitcast(FP8X4),
                        rhs_scale=xs[:, 0:P],
                        start=True,
                        stop=True,
                    )
                tiles[("cb", u, g)] = bank

        def ph_r(u):
            rg = grp.tile([P, 1024], BF16, name="g_r", align_bytes=64)
            for g in range(2):
                dst = rg[:, 512 * g : 512 * g + 512].rearrange("p (j t) -> p j t", t=4)
                src = tiles[("cb", u, g)][:].rearrange("p t j -> p j t")
                nc.scalar.activation(out=dst, in_=src, func=ACT.Relu)
            tiles[("rg", u)] = rg

        def ph_qr(u):
            rc = cod.tile([P, 256], U32, name="c_r", align_bytes=64, bufs=O_D - O_QR + 2)
            rs = cod.tile([P, 256], U8, name="s_r", align_bytes=64, bufs=O_D - O_QR + 2)
            quantise(rc[:], rs[:], tiles[("rg", u)][:])
            tiles[("rc", u)] = rc
            tiles[("rs", u)] = rs

        def ph_d(u):
            rc, rs = tiles[("rc", u)], tiles[("rs", u)]
            sc, ss = tiles[("cxs", u)], tiles[("sxs", u)]
            acc = ps_d.tile([P, D], F32, name="db", tag="db")
            passes = ((sc, ss, P, w3c, w3s, 0), (rc, rs, 0, w2c, w2s, 0), (rc, rs, P, w2c, w2s, 512))
            for i, (lc, ls, lo, wc, ws, wo) in enumerate(passes):
                nc.tensor.matmul_mx(
                    out=acc[:],
                    lhsT=lc[:, lo : lo + P].bitcast(FP8X4),
                    lhsT_scale=ls[:, lo : lo + P],
                    rhs=wc[:, wo : wo + 512].bitcast(FP8X4),
                    rhs_scale=ws[:, wo : wo + 512],
                    start=(i == 0),
                    stop=(i == 2),
                )
            tiles[("acc", u)] = acc

        def e_slice(u, n=1):
            j = u % 2
            return tiles[("e", u - j)][:, D * j : D * (j + n)]

        def runs(u):
            if unit_group[u][0] == unit_group[u + 1][0]:
                return ((u, 2),)
            return ((u, 1), (u + 1, 1))

        def ph_b(u):
            for v in (u, u + 1):
                e = e_slice(v).rearrange("m (p n) -> m p n", n=4)
                acc = tiles[("acc", v)][:].rearrange("m (n p) -> m p n", n=4)
                nc.vector.tensor_tensor(out=e, in0=e, in1=acc, op=ALU.subtract)

        def ph_relu(u):
            if u == NU - 2:
                for v in (u, u + 1):
                    nc.scalar.activation(out=e_slice(v), in_=e_slice(v), func=ACT.Relu, scale=0.1)
                return
            e = tiles[("e", u)]
            w = RV_LATE if u >= LATE else RV
            nc.scalar.activation(out=e[:, w:], in_=e[:, w:], func=ACT.Relu, scale=0.1)
            nc.vector.tensor_scalar(out=e[:, 0:w], in0=e[:, 0:w], scalar1=0.1, scalar2=0.0, op0=ALU.mult, op1=ALU.max)

        def ph_out(spans):
            for v, n in spans:
                gi, j = unit_group[v]
                if j == 0:
                    o = epi.tile([P, GROUPS[gi] * D], F32, name="o", bufs=4)
                    tiles[("o", gi)] = o
                nc.vector.scalar_tensor_tensor(
                    out=tiles[("o", gi)][:, D * j : D * (j + n)],
                    in0=tiles[("rn", gi)][:, D * j : D * (j + n)],
                    scalar=0.9,
                    in1=e_slice(v, n),
                    op0=ALU.mult,
                    op1=ALU.add,
                )
                if j + n == GROUPS[gi]:
                    nc.sync.dma_start(out=gview(out, gi), in_=tiles[("o", gi)][:])

        load(0, "x")
        load(0, "som")
        load(1, "x")
        load(1, "som")
        load_w3()
        load_w1(0, 2)
        load_w1(2, 2)
        load_w2()
        load(0, "pr")
        load(2, "x")
        load(2, "som")
        load(1, "pr")
        load(2, "pr")
        head_loads = [(0, 'x'), (0, 'som'), (1, 'x'), (1, 'som'), (0, 'pr'), (2, 'x'), (2, 'som'), (1, 'pr'), (2, 'pr')]
        loads_at = {}
        for gi in range(len(GROUPS)):
            for which in ("x", "som", "pr", "rn"):
                if (gi, which) in head_loads:
                    continue
                k = first[gi] + FIRST_USE[which] - LEAD
                old = gi - NBUF[which]
                if old >= 0:
                    k = max(k, first[old] + GROUPS[old] - 1 + LAST_USE[which] + 1)
                k = max(k, 0)
                if k not in loads_at:
                    loads_at[k] = []
                loads_at[k].append((gi, which))

        for k in range(0, NU + 9):
            for gi, which in loads_at.get(k, []):
                load(gi, which)
            if ok(k - 1):
                ph_tc(k - 1)
            if ok(k - 5):
                ph_d(k - 5)
            if ok(k - 2):
                ph_c(k - 2)
            if k % 2 == 0:
                for u in (k, k + 1):
                    if ok(u):
                        ph_t(u)
            if (k - 7) % 2 == 0 and ok(k - 7):
                ph_relu(k - 7)
            if ok(k - 3):
                ph_r(k - 3)
            if ok(k - 4):
                ph_qr(k - 4)
            if (k - 6) % 2 == 0 and ok(k - 6):
                ph_b(k - 6)
            if ok(k - 1):
                ph_q(k - 1)
            if 0 <= k - 2 < 2 * E_PAIRS:
                u = k - 2
                ph_a(u // 2 * 2, D * (u % 2), D * (u % 2) + D, nc.vector)
            if (k - 7) % 2 == 0 and ok(k - 7):
                ph_out(((k - 7, 1),) if k - 7 == NU - 4 else runs(k - 7))
            if k - 8 == NU - 4:
                ph_out(((NU - 3, 1),))
            if AV < 2 * D and (k - 1) % 2 == 0 and 2 * E_PAIRS <= k - 1 < NU:
                ph_a(k - 1, AV, 2 * D, nc.gpsimd)
            if (k - 2) % 2 == 0 and 2 * E_PAIRS <= k - 2 < NU:
                ph_a(k - 2, 0, AV, nc.vector)
            if k == 0:
                w_t("w3", 0, 0)
                w_t("w3", 0, 1)
                w_c("w3", 0, 0, True)
                w_c("w3", 0, 1, False)
            if k == 1:
                w_t("w1", 0, 0)
                w_t("w1", 0, 1)
                w_t("w1", 1, 0)
                w_t("w1", 1, 1)
                w_c("w1", 0, 0, True)
                w_c("w1", 0, 1, False)
                w_q("w1", 0)
                w_c("w1", 1, 0, True)
                w_c("w1", 1, 1, False)
                w_q("w1", 1)
                w_q("w3", 0)
                w_t("w2", 0, 0)
                w_t("w2", 0, 1)
            if k == 2:
                w_c("w2", 0, 0, True)
                w_c("w2", 0, 1, False)
                w_q("w2", 0)
                w_t("w2", 1, 0)
                w_t("w2", 1, 1)
            if k == 3:
                w_c("w2", 1, 0, True)
                w_c("w2", 1, 1, False)
                w_q("w2", 1)
